import numpy as np
import ml_dtypes


def mxq(x, axis, fmt="e4m3"):
    dtype, down = {"e4m3": (ml_dtypes.float8_e4m3fn, 7), "e5m2": (ml_dtypes.float8_e5m2, 14)}[fmt]
    v = np.moveaxis(np.asarray(x, np.float32).astype(ml_dtypes.bfloat16).astype(np.float64), axis, -1)
    blocks = v.reshape(v.shape[:-1] + (-1, 32))
    amax = np.abs(blocks).max(-1, keepdims=True)
    byte = np.maximum(np.where(amax > 0, np.frexp(amax)[1] - 1 + 127, 0) - down, 1)
    scale = np.exp2(byte - 127.0)
    codes = (blocks / scale).astype(np.float32).astype(dtype).astype(np.float64)
    return np.moveaxis((codes * scale).reshape(v.shape), -1, axis)


WIDE = False


def mx_kscale(k, group=512):
    if not WIDE:
        return np.ones(k)
    levels = np.array([10, -10, 5, -5, 0])
    if group != 512:
        return np.exp2(np.random.permutation(np.resize(levels, k // group))).repeat(group)
    if k % 512:
        return np.exp2(np.random.permutation(np.resize(levels, k // 32))).repeat(32)
    a = np.empty((k // 512, 16))
    for p in range(k // 512):
        a[p, :8] = np.random.permutation(np.resize(levels, 8))
        for g in range(8):
            far = levels[np.abs(levels - a[p, g]) >= 10]
            a[p, g + 8] = far[np.random.randint(len(far))]
    return np.exp2(a.ravel()).repeat(32)


BF16 = ml_dtypes.bfloat16


def bf(x):
    return np.asarray(x, np.float32).astype(BF16)


def f64(x):
    return np.asarray(x).astype(np.float64)


N, D, C = 512, 4096, 4


def unit(v):
    return v / np.linalg.norm(v, axis=-1, keepdims=True)


def cnormal(*shape):
    return np.random.standard_normal(shape) + 1j * np.random.standard_normal(shape)


def draw_states():
    centre = unit(unit(cnormal(D)) + unit(cnormal(C, D)))
    label = np.random.randint(0, C, N)
    a2 = np.where(np.random.random(N) < 0.5, 0.95, 0.65)[:, None]
    psi = np.sqrt(a2) * centre[label] + np.sqrt(1.0 - a2) * unit(cnormal(N, D))
    theta = 2.0 * np.pi * np.random.random(N)[:, None]
    return unit(psi * np.exp(1j * theta))


def setup_inputs():
    s = mx_kscale(N, 128)
    psi = draw_states()
    r0 = bf(psi.real)
    i0 = bf(psi.imag)
    g = np.random.standard_normal((N, N)) * np.exp2(np.random.randint(-6, 1, (N, 1))) * 16.0
    g = bf(g / (s[:, None] * s[None, :]))
    rf, jf = f64(r0), f64(i0)
    g_re = rf @ rf.T + jf @ jf.T
    g_im = jf @ rf.T - rf @ jf.T
    return {"latent_re": bf(rf * s[:, None]), "latent_im": bf(jf * s[:, None]),
            "g_re": np.asarray(g_re, np.float32), "g_im": np.asarray(g_im, np.float32), "grad_out": g}


def reference(latent_re, latent_im, g_re, g_im, grad_out):
    g = f64(grad_out)
    sym = g + g.T
    p = 2.0 * sym * f64(g_re)
    q = -2.0 * sym * f64(g_im)
    pq = mxq(p, 1, "e5m2")
    qq = mxq(q, 1, "e5m2")
    rq = mxq(f64(latent_re), 0, "e4m3")
    iq = mxq(f64(latent_im), 0, "e4m3")
    d_re = (pq @ rq) + (qq @ iq)
    d_im = (pq @ iq) - (qq @ rq)
    return d_re, d_im

@@ -1,0 +1,229 @@
+from contextlib import ExitStack
+
+import concourse.mybir as mybir
+from concourse.masks import make_identity
+
+FLOPS = 4 * 2 * 512 * 512 * 4096
+
+F32 = mybir.dt.float32
+BF16 = mybir.dt.bfloat16
+U32 = mybir.dt.uint32
+U8 = mybir.dt.uint8
+E4X4 = mybir.dt.float8_e4m3fn_x4
+E5X4 = mybir.dt.float8_e5m2_x4
+ALU = mybir.AluOpType
+
+P = 128
+PACK = 4
+STATES = 512
+DIM = 4096
+COL = 512
+N_COLS = DIM // COL
+CHUNKS = ((0, 1024), (1024, 1024), (2048, 2048))
+PAIR = 2 * COL
+V_BANKS = ((), (), (), (), (5,), (5,), (1, 3, 5, 7), (1, 3, 5, 7))
+
+
+def tile_quantumgraphneuralnetwork_pa_v_kernel(tc, latent_re, latent_im, g_re, g_im, grad_out, out_0, out_1):
+    nc = tc.nc
+    with ExitStack() as ctx:
+        ctx.enter_context(tc.manual_schedule())
+        keep = ctx.enter_context(tc.tile_pool(name="keep", bufs=1))
+        raw = ctx.enter_context(tc.tile_pool(name="raw", bufs=1))
+        stage = ctx.enter_context(tc.tile_pool(name="stage", bufs=6))
+        psum = ctx.enter_context(tc.psum_pool(name="psum", bufs=8))
+
+        lat_view = (
+            latent_re.rearrange("(p t) d -> p t d", t=PACK),
+            latent_im.rearrange("(p t) d -> p t d", t=PACK),
+        )
+        out_view = (
+            out_0.rearrange("(m t) d -> m t d", t=PACK),
+            out_1.rearrange("(m t) d -> m t d", t=PACK),
+        )
+
+        lat_codes = ([], [])
+        lat_scales = ([], [])
+        for c in range(N_COLS):
+            for s in range(2):
+                codes = keep.tile([P, COL], U32, name="lc%d_%d" % (s, c), align_bytes=64)
+                scales = keep.tile([P, COL], U8, name="ls%d_%d" % (s, c), align_bytes=64)
+                lat_codes[s].append(codes)
+                lat_scales[s].append(scales)
+        grad_codes = []
+        grad_scales = []
+        for x in range(3):
+            codes = keep.tile([P, STATES], U32, name="gc%d" % x, align_bytes=64)
+            scales = keep.tile([P, STATES], U8, name="gs%d" % x, align_bytes=64)
+            grad_codes.append(codes)
+            grad_scales.append(scales)
+
+        lat_raw = ([], [])
+        staged = {}
+
+        def raw_column(s, c):
+            for k, (start, width) in enumerate(CHUNKS):
+                if start <= c * COL < start + width:
+                    return lat_raw[s][k][:, :, c * COL - start : (c + 1) * COL - start]
+            raise ValueError("no chunk holds this column")
+
+        def interleave(copy, s, c):
+            grouped = stage.tile([P, COL, PACK], BF16, name="grouped", align_bytes=64)
+            copy(out=grouped[:], in_=raw_column(s, c).rearrange("p t w -> p w t"))
+            staged[(s, c)] = grouped
+
+        def quantize_latent(s, c):
+            nc.vector.quantize_mx(
+                out=lat_codes[s][c][:].bitcast(E4X4),
+                scales=lat_scales[s][c][:],
+                in_=staged[(s, c)][:].rearrange("p w t -> p (w t)"),
+            )
+
+        def quantize_grad(x):
+            nc.vector.quantize_mx(
+                out=grad_codes[x][:].bitcast(E5X4),
+                scales=grad_scales[x][:],
+                in_=staged[("g", x)][:].rearrange("p w t -> p (w t)"),
+            )
+
+        with tc.tile_pool(name="head", bufs=1) as head:
+            g_sb = head.tile([P, PACK, STATES], BF16, name="g_sb")
+            gim_sb = head.tile([P, PACK, STATES], F32, name="gim_sb")
+            gre_sb = head.tile([P, PACK, STATES], F32, name="gre_sb")
+            nc.sync.dma_start(out=g_sb[:], in_=grad_out.rearrange("(p t) j -> p t j", t=PACK))
+            nc.sync.dma_start(out=gim_sb[:], in_=g_im.rearrange("(p t) j -> p t j", t=PACK))
+            nc.sync.dma_start(out=gre_sb[:], in_=g_re.rearrange("(p t) j -> p t j", t=PACK))
+            for k, (start, width) in enumerate(CHUNKS):
+                for s in range(2):
+                    chunk = raw.tile([P, PACK, width], BF16, name="raw%d_%d" % (s, k))
+                    nc.sync.dma_start(out=chunk[:], in_=lat_view[s][:, :, start : start + width])
+                    lat_raw[s].append(chunk)
+
+            ident = keep.tile([P, P], F32, name="ident")
+            make_identity(nc, ident[:])
+            warm_in = keep.tile([P, 8], F32, name="warm_in")
+            warm_out = keep.tile([P, 8], F32, name="warm_out")
+            nc.vector.memset(warm_in[:], 0.0)
+            nc.scalar.copy(out=warm_out[:], in_=warm_in[:])
+
+            g_words = g_sb[:].rearrange("p t j -> p (t j)").bitcast(F32)
+            sym = []
+            for u in range(2):
+                gt = psum.tile([P, COL], F32, name="bank")
+                for tj in range(PACK):
+                    nc.tensor.transpose(
+                        gt[:, tj * P : (tj + 1) * P],
+                        g_words[:, 256 * tj + u : 256 * (tj + 1) : 2],
+                        ident[:],
+                    )
+                sym_u = head.tile([P, 2, STATES], F32, name="sym%d" % u)
+                nc.vector.tensor_tensor(
+                    out=sym_u[:].rearrange("p e (pj tj) -> p e pj tj", tj=PACK),
+                    in0=g_sb[:, 2 * u : 2 * u + 2, :].rearrange("p e (pj tj) -> p e pj tj", tj=PACK),
+                    in1=gt[:].bitcast(BF16).rearrange("p (tj pj e) -> p e pj tj", tj=PACK, e=2),
+                    op=ALU.add,
+                )
+                sym.append(sym_u)
+
+            def gradient(x, factor, saved):
+                grouped = stage.tile([P, STATES, PACK], BF16, name="grouped", align_bytes=64)
+                staged[("g", x)] = grouped
+                grouped_words = grouped[:].rearrange("p w t -> p (w t)").bitcast(F32).rearrange("p (c u) -> p c u", u=2)
+                for h in range(2):
+                    val = head.tile([P, 2, STATES], BF16, name="val%d_%d" % (x, h))
+                    nc.vector.scalar_tensor_tensor(
+                        out=val[:],
+                        in0=sym[h][:],
+                        scalar=factor,
+                        in1=saved[:, 2 * h : 2 * h + 2, :],
+                        op0=ALU.mult,
+                        op1=ALU.mult,
+                    )
+                    words = val[:].rearrange("p e j -> p (e j)").bitcast(F32)
+                    xt = psum.tile([P, 2, 2 * P], F32, name="bank")
+                    for e in range(2):
+                        for u in range(2):
+                            nc.tensor.transpose(
+                                xt[:, u, e * P : (e + 1) * P],
+                                words[:, 256 * e + u : 256 * (e + 1) : 2],
+                                ident[:],
+                            )
+                    nc.scalar.copy(
+                        out=grouped_words[:, 2 * P * h : 2 * P * (h + 1), :],
+                        in_=xt[:].rearrange("p u c -> p c u"),
+                    )
+
+            gradient(1, -2.0, gim_sb)
+            interleave(nc.scalar.copy, 0, 0)
+            gradient(2, 2.0, gim_sb)
+            gradient(0, 2.0, gre_sb)
+            interleave(nc.vector.tensor_copy, 1, 0)
+            quantize_grad(1)
+            quantize_grad(2)
+            quantize_latent(0, 0)
+            quantize_grad(0)
+            quantize_latent(1, 0)
+            interleave(nc.scalar.copy, 0, 1)
+
+        outp = ctx.enter_context(tc.tile_pool(name="outp", bufs=5))
+
+        def prepare(c):
+            if (0, c) not in staged:
+                interleave(nc.vector.tensor_copy, 0, c)
+            interleave(nc.vector.tensor_copy, 1, c)
+            quantize_latent(0, c)
+            quantize_latent(1, c)
+
+        groups = [((0,), (0, 1)), ((1,), (0, 1))]
+        for k in range(1, N_COLS // 2):
+            for o in range(2):
+                groups.append(((2 * k, 2 * k + 1), (o,)))
+
+        out_tiles = {}
+        for gi, (cols, outs) in enumerate(groups):
+            if gi + 1 < N_COLS:
+                prepare(gi + 1)
+            bank_no = 0
+            for c in cols:
+                for t in range(PACK):
+                    rows = slice(t * P, (t + 1) * P)
+                    for o in outs:
+                        key = (c // 2, o)
+                        if key not in out_tiles:
+                            result = outp.tile([P, PACK, PAIR], F32, name="result")
+                            out_tiles[key] = result
+                        acc = psum.tile([P, COL], F32, name="bank")
+                        second = 1 + o
+                        nc.tensor.matmul_mx(
+                            out=acc[:],
+                            lhsT=grad_codes[0][:, rows].bitcast(E5X4),
+                            lhsT_scale=grad_scales[0][:, rows],
+                            rhs=lat_codes[o][c][:].bitcast(E4X4),
+                            rhs_scale=lat_scales[o][c][:],
+                            start=True,
+                            stop=False,
+                        )
+                        nc.tensor.matmul_mx(
+                            out=acc[:],
+                            lhsT=grad_codes[second][:, rows].bitcast(E5X4),
+                            lhsT_scale=grad_scales[second][:, rows],
+                            rhs=lat_codes[1 - o][c][:].bitcast(E4X4),
+                            rhs_scale=lat_scales[1 - o][c][:],
+                            start=False,
+                            stop=True,
+                        )
+                        lo = (c % 2) * COL
+                        dst = out_tiles[key][:, t, lo : lo + COL]
+                        if bank_no in V_BANKS[gi]:
+                            nc.vector.tensor_copy(out=dst, in_=acc[:])
+                        else:
+                            nc.scalar.copy(out=dst, in_=acc[:])
+                        bank_no += 1
+            for o in outs:
+                first = cols[0]
+                width = len(cols) * COL
+                lo = (first % 2) * COL
+                nc.sync.dma_start(
+                    out=out_view[o][:, :, first * COL : first * COL + width],
+                    in_=out_tiles[(first // 2, o)][:, :, lo : lo + width],
+                )

@@ -20,8 +20,9 @@ DIM = 4096
 COL = 512
 N_COLS = DIM // COL
 CHUNKS = ((0, 1024), (1024, 1024), (2048, 2048))
-PAIR = 2 * COL
-V_BANKS = ((), (), (), (), (5,), (5,), (1, 3, 5, 7), (1, 3, 5, 7))
+UNITS = ((0, 0, 2), (1, 0, 3), (0, 2, 5), (1, 3, 6), (0, 5, 8), (1, 6, 8))
+MAX_UNIT_COLS = 3
+V_FROM_BANK = 44
 
 
 def tile_quantumgraphneuralnetwork_pa_v_kernel(tc, latent_re, latent_im, g_re, g_im, grad_out, out_0, out_1):
@@ -165,65 +166,48 @@ def tile_quantumgraphneuralnetwork_pa_v_kernel(tc, latent_re, latent_im, g_re, g
             quantize_latent(1, 0)
             interleave(nc.scalar.copy, 0, 1)
 
-        outp = ctx.enter_context(tc.tile_pool(name="outp", bufs=5))
+        outp = ctx.enter_context(tc.tile_pool(name="outp", bufs=14))
 
-        def prepare(c):
+        for c in range(1, N_COLS):
             if (0, c) not in staged:
                 interleave(nc.vector.tensor_copy, 0, c)
             interleave(nc.vector.tensor_copy, 1, c)
             quantize_latent(0, c)
             quantize_latent(1, c)
 
-        groups = [((0,), (0, 1)), ((1,), (0, 1))]
-        for k in range(1, N_COLS // 2):
-            for o in range(2):
-                groups.append(((2 * k, 2 * k + 1), (o,)))
-
-        out_tiles = {}
-        for gi, (cols, outs) in enumerate(groups):
-            if gi + 1 < N_COLS:
-                prepare(gi + 1)
-            bank_no = 0
-            for c in cols:
-                for t in range(PACK):
-                    rows = slice(t * P, (t + 1) * P)
-                    for o in outs:
-                        key = (c // 2, o)
-                        if key not in out_tiles:
-                            result = outp.tile([P, PACK, PAIR], F32, name="result")
-                            out_tiles[key] = result
-                        acc = psum.tile([P, COL], F32, name="bank")
-                        second = 1 + o
-                        nc.tensor.matmul_mx(
-                            out=acc[:],
-                            lhsT=grad_codes[0][:, rows].bitcast(E5X4),
-                            lhsT_scale=grad_scales[0][:, rows],
-                            rhs=lat_codes[o][c][:].bitcast(E4X4),
-                            rhs_scale=lat_scales[o][c][:],
-                            start=True,
-                            stop=False,
-                        )
-                        nc.tensor.matmul_mx(
-                            out=acc[:],
-                            lhsT=grad_codes[second][:, rows].bitcast(E5X4),
-                            lhsT_scale=grad_scales[second][:, rows],
-                            rhs=lat_codes[1 - o][c][:].bitcast(E4X4),
-                            rhs_scale=lat_scales[1 - o][c][:],
-                            start=False,
-                            stop=True,
-                        )
-                        lo = (c % 2) * COL
-                        dst = out_tiles[key][:, t, lo : lo + COL]
-                        if bank_no in V_BANKS[gi]:
-                            nc.vector.tensor_copy(out=dst, in_=acc[:])
-                        else:
-                            nc.scalar.copy(out=dst, in_=acc[:])
-                        bank_no += 1
-            for o in outs:
-                first = cols[0]
-                width = len(cols) * COL
-                lo = (first % 2) * COL
+        bank_no = 0
+        for o, c_from, c_to in UNITS:
+            second = 1 + o
+            for t in range(PACK):
+                rows = slice(t * P, (t + 1) * P)
+                row = outp.tile([P, MAX_UNIT_COLS * COL], F32, name="row")
+                for c in range(c_from, c_to):
+                    acc = psum.tile([P, COL], F32, name="bank")
+                    nc.tensor.matmul_mx(
+                        out=acc[:],
+                        lhsT=grad_codes[0][:, rows].bitcast(E5X4),
+                        lhsT_scale=grad_scales[0][:, rows],
+                        rhs=lat_codes[o][c][:].bitcast(E4X4),
+                        rhs_scale=lat_scales[o][c][:],
+                        start=True,
+                        stop=False,
+                    )
+                    nc.tensor.matmul_mx(
+                        out=acc[:],
+                        lhsT=grad_codes[second][:, rows].bitcast(E5X4),
+                        lhsT_scale=grad_scales[second][:, rows],
+                        rhs=lat_codes[1 - o][c][:].bitcast(E4X4),
+                        rhs_scale=lat_scales[1 - o][c][:],
+                        start=False,
+                        stop=True,
+                    )
+                    dst = row[:, (c - c_from) * COL : (c - c_from + 1) * COL]
+                    if bank_no >= V_FROM_BANK and bank_no % 2 == 1:
+                        nc.vector.tensor_copy(out=dst, in_=acc[:])
+                    else:
+                        nc.scalar.copy(out=dst, in_=acc[:])
+                    bank_no += 1
                 nc.sync.dma_start(
-                    out=out_view[o][:, :, first * COL : first * COL + width],
-                    in_=out_tiles[(first // 2, o)][:, :, lo : lo + width],
+                    out=out_view[o][:, t, c_from * COL : c_to * COL],
+                    in_=row[:, 0 : (c_to - c_from) * COL],
                 )

@@ -19,7 +19,8 @@ STATES = 512
 DIM = 4096
 COL = 512
 N_COLS = DIM // COL
-CHUNKS = ((0, 1024), (1024, 1024), (2048, 2048))
+CHUNKS = ((0, 1536), (1536, 2560))
+WARM_MATMULS = 7
 UNITS = ((0, 0, 2), (1, 0, 3), (0, 2, 5), (1, 3, 6), (0, 5, 8), (1, 6, 8))
 MAX_UNIT_COLS = 3
 V_FROM_BANK = 44
@@ -158,9 +159,12 @@ def tile_quantumgraphneuralnetwork_pa_v_kernel(tc, latent_re, latent_im, g_re, g
             interleave(nc.scalar.copy, 0, 0)
             gradient(2, 2.0, gim_sb)
             gradient(0, 2.0, gre_sb)
-            interleave(nc.vector.tensor_copy, 1, 0)
+            warm_bank = psum.tile([P, COL], F32, name="bank")
+            for i in range(WARM_MATMULS):
+                nc.tensor.matmul(warm_bank[:], lhsT=g_sb[:, 0, 0:P], rhs=g_sb[:, 1, :], start=True, stop=True)
             quantize_grad(1)
             quantize_grad(2)
+            interleave(nc.vector.tensor_copy, 1, 0)
             quantize_latent(0, 0)
             quantize_grad(0)
             quantize_latent(1, 0)

@@ -19,8 +19,8 @@ STATES = 512
 DIM = 4096
 COL = 512
 N_COLS = DIM // COL
-CHUNKS = ((0, 1536), (1536, 2560))
-WARM_MATMULS = 7
+CHUNKS = ((0, 1024), (1024, 1024), (2048, 2048))
+WARM_MATMULS = 6
 UNITS = ((0, 0, 2), (1, 0, 3), (0, 2, 5), (1, 3, 6), (0, 5, 8), (1, 6, 8))
 MAX_UNIT_COLS = 3
 V_FROM_BANK = 44
@@ -162,9 +162,9 @@ def tile_quantumgraphneuralnetwork_pa_v_kernel(tc, latent_re, latent_im, g_re, g
             warm_bank = psum.tile([P, COL], F32, name="bank")
             for i in range(WARM_MATMULS):
                 nc.tensor.matmul(warm_bank[:], lhsT=g_sb[:, 0, 0:P], rhs=g_sb[:, 1, :], start=True, stop=True)
+            interleave(nc.vector.tensor_copy, 1, 0)
             quantize_grad(1)
             quantize_grad(2)
-            interleave(nc.vector.tensor_copy, 1, 0)
             quantize_latent(0, 0)
             quantize_grad(0)
             quantize_latent(1, 0)

from contextlib import ExitStack

import concourse.mybir as mybir
from concourse.masks import make_identity

FLOPS = 4 * 2 * 512 * 512 * 4096

F32 = mybir.dt.float32
BF16 = mybir.dt.bfloat16
U32 = mybir.dt.uint32
U8 = mybir.dt.uint8
E4X4 = mybir.dt.float8_e4m3fn_x4
E5X4 = mybir.dt.float8_e5m2_x4
ALU = mybir.AluOpType

P = 128
PACK = 4
STATES = 512
DIM = 4096
COL = 512
N_COLS = DIM // COL
CHUNKS = ((0, 1024), (1024, 1024), (2048, 2048))
WARM_MATMULS = 6
UNITS = ((0, 0, 2), (1, 0, 3), (0, 2, 5), (1, 3, 6), (0, 5, 8), (1, 6, 8))
MAX_UNIT_COLS = 3
V_FROM_BANK = 44


def tile_quantumgraphneuralnetwork_pa_v_kernel(tc, latent_re, latent_im, g_re, g_im, grad_out, out_0, out_1):
    nc = tc.nc
    with ExitStack() as ctx:
        ctx.enter_context(tc.manual_schedule())
        keep = ctx.enter_context(tc.tile_pool(name="keep", bufs=1))
        raw = ctx.enter_context(tc.tile_pool(name="raw", bufs=1))
        stage = ctx.enter_context(tc.tile_pool(name="stage", bufs=6))
        psum = ctx.enter_context(tc.psum_pool(name="psum", bufs=8))

        lat_view = (
            latent_re.rearrange("(p t) d -> p t d", t=PACK),
            latent_im.rearrange("(p t) d -> p t d", t=PACK),
        )
        out_view = (
            out_0.rearrange("(m t) d -> m t d", t=PACK),
            out_1.rearrange("(m t) d -> m t d", t=PACK),
        )

        lat_codes = ([], [])
        lat_scales = ([], [])
        for c in range(N_COLS):
            for s in range(2):
                codes = keep.tile([P, COL], U32, name="lc%d_%d" % (s, c), align_bytes=64)
                scales = keep.tile([P, COL], U8, name="ls%d_%d" % (s, c), align_bytes=64)
                lat_codes[s].append(codes)
                lat_scales[s].append(scales)
        grad_codes = []
        grad_scales = []
        for x in range(3):
            codes = keep.tile([P, STATES], U32, name="gc%d" % x, align_bytes=64)
            scales = keep.tile([P, STATES], U8, name="gs%d" % x, align_bytes=64)
            grad_codes.append(codes)
            grad_scales.append(scales)

        lat_raw = ([], [])
        staged = {}

        def raw_column(s, c):
            for k, (start, width) in enumerate(CHUNKS):
                if start <= c * COL < start + width:
                    return lat_raw[s][k][:, :, c * COL - start : (c + 1) * COL - start]
            raise ValueError("no chunk holds this column")

        def interleave(copy, s, c):
            grouped = stage.tile([P, COL, PACK], BF16, name="grouped", align_bytes=64)
            copy(out=grouped[:], in_=raw_column(s, c).rearrange("p t w -> p w t"))
            staged[(s, c)] = grouped

        def quantize_latent(s, c):
            nc.vector.quantize_mx(
                out=lat_codes[s][c][:].bitcast(E4X4),
                scales=lat_scales[s][c][:],
                in_=staged[(s, c)][:].rearrange("p w t -> p (w t)"),
            )

        def quantize_grad(x):
            nc.vector.quantize_mx(
                out=grad_codes[x][:].bitcast(E5X4),
                scales=grad_scales[x][:],
                in_=staged[("g", x)][:].rearrange("p w t -> p (w t)"),
            )

        with tc.tile_pool(name="head", bufs=1) as head:
            g_sb = head.tile([P, PACK, STATES], BF16, name="g_sb")
            gim_sb = head.tile([P, PACK, STATES], F32, name="gim_sb")
            gre_sb = head.tile([P, PACK, STATES], F32, name="gre_sb")
            nc.sync.dma_start(out=g_sb[:], in_=grad_out.rearrange("(p t) j -> p t j", t=PACK))
            nc.sync.dma_start(out=gim_sb[:], in_=g_im.rearrange("(p t) j -> p t j", t=PACK))
            nc.sync.dma_start(out=gre_sb[:], in_=g_re.rearrange("(p t) j -> p t j", t=PACK))
            for k, (start, width) in enumerate(CHUNKS):
                for s in range(2):
                    chunk = raw.tile([P, PACK, width], BF16, name="raw%d_%d" % (s, k))
                    nc.sync.dma_start(out=chunk[:], in_=lat_view[s][:, :, start : start + width])
                    lat_raw[s].append(chunk)

            ident = keep.tile([P, P], F32, name="ident")
            make_identity(nc, ident[:])
            warm_in = keep.tile([P, 8], F32, name="warm_in")
            warm_out = keep.tile([P, 8], F32, name="warm_out")
            nc.vector.memset(warm_in[:], 0.0)
            nc.scalar.copy(out=warm_out[:], in_=warm_in[:])

            g_words = g_sb[:].rearrange("p t j -> p (t j)").bitcast(F32)
            sym = []
            for u in range(2):
                gt = psum.tile([P, COL], F32, name="bank")
                for tj in range(PACK):
                    nc.tensor.transpose(
                        gt[:, tj * P : (tj + 1) * P],
                        g_words[:, 256 * tj + u : 256 * (tj + 1) : 2],
                        ident[:],
                    )
                sym_u = head.tile([P, 2, STATES], F32, name="sym%d" % u)
                nc.vector.tensor_tensor(
                    out=sym_u[:].rearrange("p e (pj tj) -> p e pj tj", tj=PACK),
                    in0=g_sb[:, 2 * u : 2 * u + 2, :].rearrange("p e (pj tj) -> p e pj tj", tj=PACK),
                    in1=gt[:].bitcast(BF16).rearrange("p (tj pj e) -> p e pj tj", tj=PACK, e=2),
                    op=ALU.add,
                )
                sym.append(sym_u)

            def gradient(x, factor, saved):
                grouped = stage.tile([P, STATES, PACK], BF16, name="grouped", align_bytes=64)
                staged[("g", x)] = grouped
                grouped_words = grouped[:].rearrange("p w t -> p (w t)").bitcast(F32).rearrange("p (c u) -> p c u", u=2)
                for h in range(2):
                    val = head.tile([P, 2, STATES], BF16, name="val%d_%d" % (x, h))
                    nc.vector.scalar_tensor_tensor(
                        out=val[:],
                        in0=sym[h][:],
                        scalar=factor,
                        in1=saved[:, 2 * h : 2 * h + 2, :],
                        op0=ALU.mult,
                        op1=ALU.mult,
                    )
                    words = val[:].rearrange("p e j -> p (e j)").bitcast(F32)
                    xt = psum.tile([P, 2, 2 * P], F32, name="bank")
                    for e in range(2):
                        for u in range(2):
                            nc.tensor.transpose(
                                xt[:, u, e * P : (e + 1) * P],
                                words[:, 256 * e + u : 256 * (e + 1) : 2],
                                ident[:],
                            )
                    nc.scalar.copy(
                        out=grouped_words[:, 2 * P * h : 2 * P * (h + 1), :],
                        in_=xt[:].rearrange("p u c -> p c u"),
                    )

            gradient(1, -2.0, gim_sb)
            interleave(nc.scalar.copy, 0, 0)
            gradient(2, 2.0, gim_sb)
            gradient(0, 2.0, gre_sb)
            warm_bank = psum.tile([P, COL], F32, name="bank")
            for i in range(WARM_MATMULS):
                nc.tensor.matmul(warm_bank[:], lhsT=g_sb[:, 0, 0:P], rhs=g_sb[:, 1, :], start=True, stop=True)
            interleave(nc.vector.tensor_copy, 1, 0)
            quantize_grad(1)
            quantize_grad(2)
            quantize_latent(0, 0)
            quantize_grad(0)
            quantize_latent(1, 0)
            interleave(nc.scalar.copy, 0, 1)

        outp = ctx.enter_context(tc.tile_pool(name="outp", bufs=14))

        for c in range(1, N_COLS):
            if (0, c) not in staged:
                interleave(nc.vector.tensor_copy, 0, c)
            interleave(nc.vector.tensor_copy, 1, c)
            quantize_latent(0, c)
            quantize_latent(1, c)

        bank_no = 0
        for o, c_from, c_to in UNITS:
            second = 1 + o
            for t in range(PACK):
                rows = slice(t * P, (t + 1) * P)
                row = outp.tile([P, MAX_UNIT_COLS * COL], F32, name="row")
                for c in range(c_from, c_to):
                    acc = psum.tile([P, COL], F32, name="bank")
                    nc.tensor.matmul_mx(
                        out=acc[:],
                        lhsT=grad_codes[0][:, rows].bitcast(E5X4),
                        lhsT_scale=grad_scales[0][:, rows],
                        rhs=lat_codes[o][c][:].bitcast(E4X4),
                        rhs_scale=lat_scales[o][c][:],
                        start=True,
                        stop=False,
                    )
                    nc.tensor.matmul_mx(
                        out=acc[:],
                        lhsT=grad_codes[second][:, rows].bitcast(E5X4),
                        lhsT_scale=grad_scales[second][:, rows],
                        rhs=lat_codes[1 - o][c][:].bitcast(E4X4),
                        rhs_scale=lat_scales[1 - o][c][:],
                        start=False,
                        stop=True,
                    )
                    dst = row[:, (c - c_from) * COL : (c - c_from + 1) * COL]
                    if bank_no >= V_FROM_BANK and bank_no % 2 == 1:
                        nc.vector.tensor_copy(out=dst, in_=acc[:])
                    else:
                        nc.scalar.copy(out=dst, in_=acc[:])
                    bank_no += 1
                nc.sync.dma_start(
                    out=out_view[o][:, t, c_from * COL : c_to * COL],
                    in_=row[:, 0 : (c_to - c_from) * COL],
                )
